import numpy as np
import ml_dtypes


def mxq(x, axis, fmt="e4m3"):
    dtype, down = {"e4m3": (ml_dtypes.float8_e4m3fn, 7), "e5m2": (ml_dtypes.float8_e5m2, 14)}[fmt]
    v = np.moveaxis(np.asarray(x, np.float32).astype(ml_dtypes.bfloat16).astype(np.float64), axis, -1)
    blocks = v.reshape(v.shape[:-1] + (-1, 32))
    amax = np.abs(blocks).max(-1, keepdims=True)
    byte = np.maximum(np.where(amax > 0, np.frexp(amax)[1] - 1 + 127, 0) - down, 1)
    scale = np.exp2(byte - 127.0)
    codes = (blocks / scale).astype(np.float32).astype(dtype).astype(np.float64)
    return np.moveaxis((codes * scale).reshape(v.shape), -1, axis)


WIDE = False


def mx_kscale(k):
    if not WIDE:
        return np.ones(k)
    levels = np.array([10, -10, 5, -5, 0])
    a = np.random.permutation(np.resize(levels, k // 512 * 4)).reshape(k // 512, 4)
    idx = np.arange(k)
    return np.exp2(a[idx // 512, idx % 128 // 32])


BF16 = ml_dtypes.bfloat16


def bf(x):
    return np.asarray(x, np.float32).astype(BF16)


def f64(x):
    return np.asarray(x).astype(np.float64)


E2M1 = np.array([0.0, 0.5, 1.0, 1.5, 2.0, 3.0, 4.0, 6.0, -0.0, -0.5, -1.0, -1.5, -2.0, -3.0, -4.0, -6.0])


def pack_weight(w, fmt):
    k, n = w.shape
    w = f64(bf(w)).reshape(k // 32, 32, n)
    amax = np.abs(w).max(1)
    if fmt == "e4m3":
        byte = np.frexp(amax)[1] - 1 + 127 - 7
    else:
        mant, ex = np.frexp(amax / 6.0)
        byte = np.where(mant > 0.5, ex, ex - 1) + 127
    byte = np.clip(np.where(amax > 0, byte, 1), 1, 254)
    scaled = (w * np.exp2(127.0 - byte)[:, None, :]).reshape(k, n).astype(np.float32)
    by_word = np.ascontiguousarray(scaled.reshape(k // 512, 128, 4, n).transpose(0, 1, 3, 2))
    if fmt == "e4m3":
        words = by_word.astype(ml_dtypes.float8_e4m3fn).view(np.uint8)
    else:
        c = by_word.astype(ml_dtypes.float4_e2m1fn).view(np.uint8) & 0xF
        words = c[..., 0::2] | (c[..., 1::2] << 4)
    return np.ascontiguousarray(words), np.ascontiguousarray(byte.astype(np.uint8).reshape(k // 512, 16, n))


def unpack_weight(words, scales, fmt):
    g, p, n, _ = words.shape
    if fmt == "e4m3":
        vals = np.ascontiguousarray(words).view(ml_dtypes.float8_e4m3fn).astype(np.float64)
    else:
        nib = np.empty((g, p, n, 4), np.uint8)
        nib[..., 0::2] = words & 0xF
        nib[..., 1::2] = words >> 4
        vals = E2M1[nib]
    vals = vals * np.repeat(np.exp2(scales.astype(np.float64) - 127.0), 8, axis=1)[..., None]
    return vals.transpose(0, 1, 3, 2).reshape(g * 512, n)

def pack4(w):
    words, scales = pack_weight(w, "e2m1")
    return words.reshape(words.shape[0], 128, -1), scales


def unpack4(words, scales):
    return unpack_weight(words.reshape(words.shape[0], 128, -1, 2), scales, "e2m1")


B, CIN, COUT, H, W = 4, 512, 512, 32, 32


def setup_inputs():
    s = mx_kscale(CIN)
    x = np.random.standard_normal((B, CIN, H, W)) * s[None, :, None, None]
    weight = np.random.uniform(-1.0, 1.0, (CIN, COUT)) * np.sqrt(3.0 / CIN) / s[:, None]
    words, scales = pack4(weight)
    return {"x": bf(x), "weight_words": words, "weight_scales": scales}


def reference(x, weight_words, weight_scales):
    wq = unpack4(weight_words, weight_scales)
    xq = mxq(f64(x), 1, "e4m3")
    return np.einsum("io,bihw->bohw", wq, xq, optimize=True)

@@ -1,0 +1,86 @@
+import concourse.mybir as mybir
+
+BF16 = mybir.dt.bfloat16
+F32 = mybir.dt.float32
+I32 = mybir.dt.int32
+U32 = mybir.dt.uint32
+U8 = mybir.dt.uint8
+FP8X4 = mybir.dt.float8_e4m3fn_x4
+FP4X4 = mybir.dt.float4_e2m1fn_x4
+
+P = 128
+PACK = 4
+B, CIN, COUT, PIX = 4, 512, 512, 1024
+N_TILE = 512
+HALVES = PIX // N_TILE
+O_TILES = COUT // P
+FLOPS = 2 * B * PIX * CIN * COUT
+
+
+def tile_simpleconvolution_kernel(tc, x, weight_words, weight_scales, out):
+    nc = tc.nc
+    with tc.tile_pool(name="keep", bufs=1) as keep, tc.psum_pool(name="acc", bufs=8) as acc:
+        w_plane = keep.tile([P, COUT], U8, name="w_plane", align_bytes=64)
+        nc.vector.memset(w_plane[:].bitcast(I32), 0)
+        w_words = keep.tile([P, 2 * COUT], U8, name="w_words", align_bytes=64)
+
+        raw = []
+        for b in range(B):
+            raw_b = keep.tile([P, PACK, PIX], BF16, name="raw%d" % b)
+            raw.append(raw_b)
+
+        def load_x(b):
+            nc.sync.dma_start(
+                out=raw[b][:].rearrange("p t w -> p (t w)"),
+                in_=x[b].rearrange("(p t) h w -> p (t h w)", t=PACK),
+            )
+
+        load_x(0)
+        nc.sync.dma_start(out=w_words[:].bitcast(I32), in_=weight_words[0].bitcast(I32))
+        for q in range(4):
+            nc.sync.dma_start(
+                out=w_plane[32 * q : 32 * q + 4, :].bitcast(I32),
+                in_=weight_scales[0, 4 * q : 4 * q + 4, :].bitcast(I32),
+            )
+        for b in range(1, B):
+            load_x(b)
+
+        for b in range(B):
+            grouped = keep.tile([P, PIX, PACK], BF16, name="grouped%d" % b, align_bytes=64)
+            codes = keep.tile([P, PIX], U32, name="codes%d" % b, align_bytes=64)
+            plane = keep.tile([P, PIX], U8, name="plane%d" % b, align_bytes=64)
+            for h in range(HALVES):
+                cols = slice(h * N_TILE, (h + 1) * N_TILE)
+                nc.vector.tensor_copy(
+                    out=grouped[:, cols, :].rearrange("p (c i) t -> p c t i", i=4),
+                    in_=raw[b][:, :, cols].rearrange("p t (c i) -> p c t i", i=4),
+                )
+            for h in range(HALVES):
+                cols = slice(h * N_TILE, (h + 1) * N_TILE)
+                nc.vector.quantize_mx(
+                    out=codes[:, cols].bitcast(FP8X4),
+                    scales=plane[:, cols],
+                    in_=grouped[:, cols, :].rearrange("p w t -> p (w t)"),
+                )
+            for ot in range(O_TILES):
+                result = keep.tile([P, PIX], F32, name="result%d_%d" % (b, ot))
+                for h in range(HALVES):
+                    cols = slice(h * N_TILE, (h + 1) * N_TILE)
+                    bank = acc.tile([P, N_TILE], F32, name="bank")
+                    nc.tensor.matmul_mx(
+                        out=bank[:],
+                        lhsT=w_words[:, 2 * P * ot : 2 * P * (ot + 1)].bitcast(FP4X4),
+                        lhsT_scale=w_plane[:, P * ot : P * (ot + 1)],
+                        rhs=codes[:, cols].bitcast(FP8X4),
+                        rhs_scale=plane[:, cols],
+                        start=True,
+                        stop=True,
+                    )
+                    if ot == 0 and h == 0:
+                        nc.vector.tensor_copy(out=result[:, cols], in_=bank[:])
+                    else:
+                        nc.scalar.copy(out=result[:, cols], in_=bank[:])
+                nc.sync.dma_start(
+                    out=out[b, P * ot : P * (ot + 1)].rearrange("o h w -> o (h w)"),
+                    in_=result[:],
+                )

@@ -63,7 +63,8 @@ def tile_simpleconvolution_kernel(tc, x, weight_words, weight_scales, out):
                     in_=grouped[:, cols, :].rearrange("p w t -> p (w t)"),
                 )
             for ot in range(O_TILES):
-                result = keep.tile([P, PIX], F32, name="result%d_%d" % (b, ot))
+                if ot % 2 == 0:
+                    result = keep.tile([P, 2, PIX], F32, name="result%d_%d" % (b, ot // 2))
                 for h in range(HALVES):
                     cols = slice(h * N_TILE, (h + 1) * N_TILE)
                     bank = acc.tile([P, N_TILE], F32, name="bank")
@@ -76,11 +77,12 @@ def tile_simpleconvolution_kernel(tc, x, weight_words, weight_scales, out):
                         start=True,
                         stop=True,
                     )
-                    if ot == 0 and h == 0:
-                        nc.vector.tensor_copy(out=result[:, cols], in_=bank[:])
+                    if h == 0 and (ot < 2 or b == B - 1):
+                        nc.vector.tensor_copy(out=result[:, ot % 2, cols], in_=bank[:])
                     else:
-                        nc.scalar.copy(out=result[:, cols], in_=bank[:])
-                nc.sync.dma_start(
-                    out=out[b, P * ot : P * (ot + 1)].rearrange("o h w -> o (h w)"),
-                    in_=result[:],
-                )
+                        nc.scalar.copy(out=result[:, ot % 2, cols], in_=bank[:])
+                if ot % 2 == 1:
+                    nc.sync.dma_start(
+                        out=out[b, P * (ot - 1) : P * (ot + 1)].rearrange("(j o) h w -> o j (h w)", j=2),
+                        in_=result[:],
+                    )

@@ -45,16 +45,23 @@ def tile_simpleconvolution_kernel(tc, x, weight_words, weight_scales, out):
         for b in range(1, B):
             load_x(b)
 
+        def regroup(copy, grouped, b, lo, hi):
+            copy(
+                out=grouped[:, lo:hi, :].rearrange("p (c i) t -> p c t i", i=4),
+                in_=raw[b][:, :, lo:hi].rearrange("p t (c i) -> p c t i", i=4),
+            )
+
         for b in range(B):
             grouped = keep.tile([P, PIX, PACK], BF16, name="grouped%d" % b, align_bytes=64)
             codes = keep.tile([P, PIX], U32, name="codes%d" % b, align_bytes=64)
             plane = keep.tile([P, PIX], U8, name="plane%d" % b, align_bytes=64)
-            for h in range(HALVES):
-                cols = slice(h * N_TILE, (h + 1) * N_TILE)
-                nc.vector.tensor_copy(
-                    out=grouped[:, cols, :].rearrange("p (c i) t -> p c t i", i=4),
-                    in_=raw[b][:, :, cols].rearrange("p t (c i) -> p c t i", i=4),
-                )
+            if b == 0:
+                regroup(nc.scalar.copy, grouped, b, 512, 768)
+                regroup(nc.vector.tensor_copy, grouped, b, 0, 512)
+                regroup(nc.vector.tensor_copy, grouped, b, 768, 1024)
+            else:
+                regroup(nc.vector.tensor_copy, grouped, b, 0, 512)
+                regroup(nc.vector.tensor_copy, grouped, b, 512, 1024)
             for h in range(HALVES):
                 cols = slice(h * N_TILE, (h + 1) * N_TILE)
                 nc.vector.quantize_mx(
@@ -63,8 +70,7 @@ def tile_simpleconvolution_kernel(tc, x, weight_words, weight_scales, out):
                     in_=grouped[:, cols, :].rearrange("p w t -> p (w t)"),
                 )
             for ot in range(O_TILES):
-                if ot % 2 == 0:
-                    result = keep.tile([P, 2, PIX], F32, name="result%d_%d" % (b, ot // 2))
+                result = keep.tile([P, PIX], F32, name="result%d_%d" % (b, ot))
                 for h in range(HALVES):
                     cols = slice(h * N_TILE, (h + 1) * N_TILE)
                     bank = acc.tile([P, N_TILE], F32, name="bank")
@@ -77,12 +83,11 @@ def tile_simpleconvolution_kernel(tc, x, weight_words, weight_scales, out):
                         start=True,
                         stop=True,
                     )
-                    if h == 0 and (ot < 2 or b == B - 1):
-                        nc.vector.tensor_copy(out=result[:, ot % 2, cols], in_=bank[:])
+                    if h == 0 and (ot == 0 or b == B - 1):
+                        nc.vector.tensor_copy(out=result[:, cols], in_=bank[:])
                     else:
-                        nc.scalar.copy(out=result[:, ot % 2, cols], in_=bank[:])
-                if ot % 2 == 1:
-                    nc.sync.dma_start(
-                        out=out[b, P * (ot - 1) : P * (ot + 1)].rearrange("(j o) h w -> o j (h w)", j=2),
-                        in_=result[:],
-                    )
+                        nc.scalar.copy(out=result[:, cols], in_=bank[:])
+                nc.sync.dma_start(
+                    out=out[b, P * ot : P * (ot + 1)].rearrange("o h w -> o (h w)"),
+                    in_=result[:],
+                )

@@ -56,9 +56,9 @@ def tile_simpleconvolution_kernel(tc, x, weight_words, weight_scales, out):
             codes = keep.tile([P, PIX], U32, name="codes%d" % b, align_bytes=64)
             plane = keep.tile([P, PIX], U8, name="plane%d" % b, align_bytes=64)
             if b == 0:
-                regroup(nc.scalar.copy, grouped, b, 512, 768)
+                regroup(nc.scalar.copy, grouped, b, 512, 848)
                 regroup(nc.vector.tensor_copy, grouped, b, 0, 512)
-                regroup(nc.vector.tensor_copy, grouped, b, 768, 1024)
+                regroup(nc.vector.tensor_copy, grouped, b, 848, 1024)
             else:
                 regroup(nc.vector.tensor_copy, grouped, b, 0, 512)
                 regroup(nc.vector.tensor_copy, grouped, b, 512, 1024)
@@ -87,7 +87,13 @@ def tile_simpleconvolution_kernel(tc, x, weight_words, weight_scales, out):
                         nc.vector.tensor_copy(out=result[:, cols], in_=bank[:])
                     else:
                         nc.scalar.copy(out=result[:, cols], in_=bank[:])
-                nc.sync.dma_start(
-                    out=out[b, P * ot : P * (ot + 1)].rearrange("o h w -> o (h w)"),
-                    in_=result[:],
-                )
+                    if b == 0 and ot == 0:
+                        nc.sync.dma_start(
+                            out=out[b, P * ot : P * (ot + 1)].rearrange("o h w -> o (h w)")[:, cols],
+                            in_=result[:, cols],
+                        )
+                if b > 0 or ot > 0:
+                    nc.sync.dma_start(
+                        out=out[b, P * ot : P * (ot + 1)].rearrange("o h w -> o (h w)"),
+                        in_=result[:],
+                    )

@@ -15,85 +15,105 @@ N_TILE = 512
 HALVES = PIX // N_TILE
 O_TILES = COUT // P
 FLOPS = 2 * B * PIX * CIN * COUT
+TILES_A_STORE = (1, 2, 2, 2)
 
 
 def tile_simpleconvolution_kernel(tc, x, weight_words, weight_scales, out):
     nc = tc.nc
-    with tc.tile_pool(name="keep", bufs=1) as keep, tc.psum_pool(name="acc", bufs=8) as acc:
+    with tc.tile_pool(name="keep", bufs=1) as keep, tc.psum_pool(name="acc", bufs=8) as acc, tc.manual_schedule():
+        s_raw = keep.tile([P, COUT], U8, name="s_raw", align_bytes=64)
+        w_raw = keep.tile([P, 2 * COUT], U8, name="w_raw", align_bytes=64)
         w_plane = keep.tile([P, COUT], U8, name="w_plane", align_bytes=64)
-        nc.vector.memset(w_plane[:].bitcast(I32), 0)
         w_words = keep.tile([P, 2 * COUT], U8, name="w_words", align_bytes=64)
-
-        raw = []
+        raw, grouped, codes, plane, result = [], [], [], [], []
         for b in range(B):
-            raw_b = keep.tile([P, PACK, PIX], BF16, name="raw%d" % b)
-            raw.append(raw_b)
+            raw.append(keep.tile([P, PACK, PIX], BF16, name="raw%d" % b))
+            grouped.append(keep.tile([P, PIX, PACK], BF16, name="grouped%d" % b, align_bytes=64))
+            codes.append(keep.tile([P, PIX], U32, name="codes%d" % b, align_bytes=64))
+            plane.append(keep.tile([P, PIX], U8, name="plane%d" % b, align_bytes=64))
+            result.append(keep.tile([P, O_TILES, PIX], F32, name="result%d" % b))
 
-        def load_x(b):
-            nc.sync.dma_start(
+        def load_x(queue, b):
+            queue.dma_start(
                 out=raw[b][:].rearrange("p t w -> p (t w)"),
                 in_=x[b].rearrange("(p t) h w -> p (t h w)", t=PACK),
             )
 
-        load_x(0)
-        nc.sync.dma_start(out=w_words[:].bitcast(I32), in_=weight_words[0].bitcast(I32))
-        for q in range(4):
-            nc.sync.dma_start(
-                out=w_plane[32 * q : 32 * q + 4, :].bitcast(I32),
-                in_=weight_scales[0, 4 * q : 4 * q + 4, :].bitcast(I32),
-            )
-        for b in range(1, B):
-            load_x(b)
-
-        def regroup(copy, grouped, b, lo, hi):
+        def regroup(copy, b, lo, hi):
             copy(
-                out=grouped[:, lo:hi, :].rearrange("p (c i) t -> p c t i", i=4),
+                out=grouped[b][:, lo:hi, :].rearrange("p (c i) t -> p c t i", i=4),
                 in_=raw[b][:, :, lo:hi].rearrange("p t (c i) -> p c t i", i=4),
             )
 
+        def quantize(b, h):
+            cols = slice(h * N_TILE, (h + 1) * N_TILE)
+            nc.vector.quantize_mx(
+                out=codes[b][:, cols].bitcast(FP8X4),
+                scales=plane[b][:, cols],
+                in_=grouped[b][:, cols, :].rearrange("p w t -> p (w t)"),
+            )
+
+        def multiply(b, j, h):
+            cols = slice(h * N_TILE, (h + 1) * N_TILE)
+            bank = acc.tile([P, N_TILE], F32, name="bank")
+            nc.tensor.matmul_mx(
+                out=bank[:],
+                lhsT=w_words[:, 2 * P * j : 2 * P * (j + 1)].bitcast(FP4X4),
+                lhsT_scale=w_plane[:, P * j : P * (j + 1)],
+                rhs=codes[b][:, cols].bitcast(FP8X4),
+                rhs_scale=plane[b][:, cols],
+                start=True,
+                stop=True,
+            )
+            return bank
+
+        def empty(copy, bank, b, j, h):
+            copy(out=result[b][:, j, h * N_TILE : (h + 1) * N_TILE], in_=bank[:])
+
+        def store(b, j_lo, j_hi):
+            out_b = out[b].rearrange("(p j) h w -> p j (h w)", j=O_TILES)
+            nc.sync.dma_start(out=out_b[:, j_lo:j_hi, :], in_=result[b][:, j_lo:j_hi, :])
+
+        load_x(nc.scalar, 0)
+        nc.sync.dma_start(out=w_raw[:].bitcast(I32), in_=weight_words[0].bitcast(I32))
+        nc.vector.memset(s_raw[:].bitcast(I32), 0)
+        for q in range(4):
+            nc.sync.dma_start(
+                out=s_raw[32 * q : 32 * q + 4, :].bitcast(I32),
+                in_=weight_scales[0, 4 * q : 4 * q + 4, :].bitcast(I32),
+            )
+        for b in range(1, B):
+            load_x(nc.sync, b)
+
+        nc.vector.tensor_copy(
+            out=w_words[:].rearrange("p (j m e) -> p j m e", j=O_TILES, e=2),
+            in_=w_raw[:].rearrange("p (m j e) -> p j m e", j=O_TILES, e=2),
+        )
+        regroup(nc.scalar.copy, 0, 768, 1024)
+        regroup(nc.vector.tensor_copy, 0, 0, 512)
+        nc.vector.tensor_copy(
+            out=w_plane[:].rearrange("p (j m) -> p j m", j=O_TILES),
+            in_=s_raw[:].rearrange("p (m j) -> p j m", j=O_TILES),
+        )
+        quantize(0, 0)
+        regroup(nc.vector.tensor_copy, 0, 512, 768)
+        quantize(0, 1)
+
         for b in range(B):
-            grouped = keep.tile([P, PIX, PACK], BF16, name="grouped%d" % b, align_bytes=64)
-            codes = keep.tile([P, PIX], U32, name="codes%d" % b, align_bytes=64)
-            plane = keep.tile([P, PIX], U8, name="plane%d" % b, align_bytes=64)
-            if b == 0:
-                regroup(nc.scalar.copy, grouped, b, 512, 848)
-                regroup(nc.vector.tensor_copy, grouped, b, 0, 512)
-                regroup(nc.vector.tensor_copy, grouped, b, 848, 1024)
-            else:
-                regroup(nc.vector.tensor_copy, grouped, b, 0, 512)
-                regroup(nc.vector.tensor_copy, grouped, b, 512, 1024)
-            for h in range(HALVES):
-                cols = slice(h * N_TILE, (h + 1) * N_TILE)
-                nc.vector.quantize_mx(
-                    out=codes[:, cols].bitcast(FP8X4),
-                    scales=plane[:, cols],
-                    in_=grouped[:, cols, :].rearrange("p w t -> p (w t)"),
-                )
-            for ot in range(O_TILES):
-                result = keep.tile([P, PIX], F32, name="result%d_%d" % (b, ot))
-                for h in range(HALVES):
-                    cols = slice(h * N_TILE, (h + 1) * N_TILE)
-                    bank = acc.tile([P, N_TILE], F32, name="bank")
-                    nc.tensor.matmul_mx(
-                        out=bank[:],
-                        lhsT=w_words[:, 2 * P * ot : 2 * P * (ot + 1)].bitcast(FP4X4),
-                        lhsT_scale=w_plane[:, P * ot : P * (ot + 1)],
-                        rhs=codes[:, cols].bitcast(FP8X4),
-                        rhs_scale=plane[:, cols],
-                        start=True,
-                        stop=True,
-                    )
-                    if h == 0 and (ot == 0 or b == B - 1):
-                        nc.vector.tensor_copy(out=result[:, cols], in_=bank[:])
+            last = b == B - 1
+            for pair in range(0, O_TILES, 2):
+                order = [(pair, 0), (pair + 1, 0), (pair, 1), (pair + 1, 1)]
+                banks = [multiply(b, j, h) for j, h in order]
+                for n, (j, h) in enumerate(order):
+                    if last:
+                        vector_takes = j % 2 == 0
                     else:
-                        nc.scalar.copy(out=result[:, cols], in_=bank[:])
-                    if b == 0 and ot == 0:
-                        nc.sync.dma_start(
-                            out=out[b, P * ot : P * (ot + 1)].rearrange("o h w -> o (h w)")[:, cols],
-                            in_=result[:, cols],
-                        )
-                if b > 0 or ot > 0:
-                    nc.sync.dma_start(
-                        out=out[b, P * ot : P * (ot + 1)].rearrange("o h w -> o (h w)"),
-                        in_=result[:],
-                    )
+                        vector_takes = b > 0 and pair == 0 and n == 0
+                    empty(nc.vector.tensor_copy if vector_takes else nc.scalar.copy, banks[n], b, j, h)
+                    if h == 1 and (j + 1) % TILES_A_STORE[b] == 0:
+                        store(b, j + 1 - TILES_A_STORE[b], j + 1)
+                if pair == 0 and not last:
+                    regroup(nc.vector.tensor_copy, b + 1, 0, 512)
+                    regroup(nc.vector.tensor_copy, b + 1, 512, 1024)
+                    quantize(b + 1, 0)
+                    quantize(b + 1, 1)

@@ -74,8 +74,8 @@ def tile_simpleconvolution_kernel(tc, x, weight_words, weight_scales, out):
             out_b = out[b].rearrange("(p j) h w -> p j (h w)", j=O_TILES)
             nc.sync.dma_start(out=out_b[:, j_lo:j_hi, :], in_=result[b][:, j_lo:j_hi, :])
 
-        load_x(nc.scalar, 0)
         nc.sync.dma_start(out=w_raw[:].bitcast(I32), in_=weight_words[0].bitcast(I32))
+        load_x(nc.sync, 0)
         nc.vector.memset(s_raw[:].bitcast(I32), 0)
         for q in range(4):
             nc.sync.dma_start(

@@ -15,7 +15,8 @@ N_TILE = 512
 HALVES = PIX // N_TILE
 O_TILES = COUT // P
 FLOPS = 2 * B * PIX * CIN * COUT
-TILES_A_STORE = (1, 2, 2, 2)
+LOADS = (2, 1, 1, 1)
+STORE_AFTER = ((0, 1, 3), (1, 3), (1, 3), (1, 3))
 
 
 def tile_simpleconvolution_kernel(tc, x, weight_words, weight_scales, out):
@@ -27,22 +28,31 @@ def tile_simpleconvolution_kernel(tc, x, weight_words, weight_scales, out):
         w_words = keep.tile([P, 2 * COUT], U8, name="w_words", align_bytes=64)
         raw, grouped, codes, plane, result = [], [], [], [], []
         for b in range(B):
-            raw.append(keep.tile([P, PACK, PIX], BF16, name="raw%d" % b))
+            raw.append([keep.tile([P, PACK, PIX // LOADS[b]], BF16, name="raw%d_%d" % (b, c)) for c in range(LOADS[b])])
             grouped.append(keep.tile([P, PIX, PACK], BF16, name="grouped%d" % b, align_bytes=64))
             codes.append(keep.tile([P, PIX], U32, name="codes%d" % b, align_bytes=64))
             plane.append(keep.tile([P, PIX], U8, name="plane%d" % b, align_bytes=64))
             result.append(keep.tile([P, O_TILES, PIX], F32, name="result%d" % b))
 
-        def load_x(queue, b):
-            queue.dma_start(
-                out=raw[b][:].rearrange("p t w -> p (t w)"),
-                in_=x[b].rearrange("(p t) h w -> p (t h w)", t=PACK),
-            )
+        def load_x(b, c):
+            width = PIX // LOADS[b]
+            if LOADS[b] == 1:
+                nc.sync.dma_start(
+                    out=raw[b][c][:].rearrange("p t w -> p (t w)"),
+                    in_=x[b].rearrange("(p t) h w -> p (t h w)", t=PACK),
+                )
+            else:
+                nc.sync.dma_start(
+                    out=raw[b][c][:],
+                    in_=x[b].rearrange("(p t) h w -> p t (h w)", t=PACK)[:, :, c * width : (c + 1) * width],
+                )
 
         def regroup(copy, b, lo, hi):
+            width = PIX // LOADS[b]
+            c = lo // width
             copy(
                 out=grouped[b][:, lo:hi, :].rearrange("p (c i) t -> p c t i", i=4),
-                in_=raw[b][:, :, lo:hi].rearrange("p t (c i) -> p c t i", i=4),
+                in_=raw[b][c][:, :, lo - c * width : hi - c * width].rearrange("p t (c i) -> p c t i", i=4),
             )
 
         def quantize(b, h):
@@ -75,28 +85,29 @@ def tile_simpleconvolution_kernel(tc, x, weight_words, weight_scales, out):
             nc.sync.dma_start(out=out_b[:, j_lo:j_hi, :], in_=result[b][:, j_lo:j_hi, :])
 
         nc.sync.dma_start(out=w_raw[:].bitcast(I32), in_=weight_words[0].bitcast(I32))
-        load_x(nc.sync, 0)
+        load_x(0, 0)
         nc.vector.memset(s_raw[:].bitcast(I32), 0)
         for q in range(4):
             nc.sync.dma_start(
                 out=s_raw[32 * q : 32 * q + 4, :].bitcast(I32),
                 in_=weight_scales[0, 4 * q : 4 * q + 4, :].bitcast(I32),
             )
+        load_x(0, 1)
         for b in range(1, B):
-            load_x(nc.sync, b)
+            load_x(b, 0)
 
         nc.vector.tensor_copy(
             out=w_words[:].rearrange("p (j m e) -> p j m e", j=O_TILES, e=2),
             in_=w_raw[:].rearrange("p (m j e) -> p j m e", j=O_TILES, e=2),
         )
-        regroup(nc.scalar.copy, 0, 768, 1024)
+        regroup(nc.scalar.copy, 0, 896, 1024)
         regroup(nc.vector.tensor_copy, 0, 0, 512)
         nc.vector.tensor_copy(
             out=w_plane[:].rearrange("p (j m) -> p j m", j=O_TILES),
             in_=s_raw[:].rearrange("p (m j) -> p j m", j=O_TILES),
         )
         quantize(0, 0)
-        regroup(nc.vector.tensor_copy, 0, 512, 768)
+        regroup(nc.vector.tensor_copy, 0, 512, 896)
         quantize(0, 1)
 
         for b in range(B):
@@ -110,8 +121,8 @@ def tile_simpleconvolution_kernel(tc, x, weight_words, weight_scales, out):
                     else:
                         vector_takes = b > 0 and pair == 0 and n == 0
                     empty(nc.vector.tensor_copy if vector_takes else nc.scalar.copy, banks[n], b, j, h)
-                    if h == 1 and (j + 1) % TILES_A_STORE[b] == 0:
-                        store(b, j + 1 - TILES_A_STORE[b], j + 1)
+                    if h == 1 and j in STORE_AFTER[b]:
+                        store(b, max([0] + [k + 1 for k in STORE_AFTER[b] if k < j]), j + 1)
                 if pair == 0 and not last:
                     regroup(nc.vector.tensor_copy, b + 1, 0, 512)
                     regroup(nc.vector.tensor_copy, b + 1, 512, 1024)

@@ -100,14 +100,15 @@ def tile_simpleconvolution_kernel(tc, x, weight_words, weight_scales, out):
             out=w_words[:].rearrange("p (j m e) -> p j m e", j=O_TILES, e=2),
             in_=w_raw[:].rearrange("p (m j e) -> p j m e", j=O_TILES, e=2),
         )
-        regroup(nc.scalar.copy, 0, 896, 1024)
-        regroup(nc.vector.tensor_copy, 0, 0, 512)
+        regroup(nc.scalar.copy, 0, 352, 512)
+        regroup(nc.scalar.copy, 0, 848, 1024)
+        regroup(nc.vector.tensor_copy, 0, 0, 352)
         nc.vector.tensor_copy(
             out=w_plane[:].rearrange("p (j m) -> p j m", j=O_TILES),
             in_=s_raw[:].rearrange("p (m j) -> p j m", j=O_TILES),
         )
         quantize(0, 0)
-        regroup(nc.vector.tensor_copy, 0, 512, 896)
+        regroup(nc.vector.tensor_copy, 0, 512, 848)
         quantize(0, 1)
 
         for b in range(B):

@@ -37,10 +37,11 @@ def tile_simpleconvolution_kernel(tc, x, weight_words, weight_scales, out):
         def load_x(b, c):
             width = PIX // LOADS[b]
             if LOADS[b] == 1:
-                nc.sync.dma_start(
-                    out=raw[b][c][:].rearrange("p t w -> p (t w)"),
-                    in_=x[b].rearrange("(p t) h w -> p (t h w)", t=PACK),
-                )
+                for odd in range(2):
+                    nc.sync.dma_start(
+                        out=raw[b][c][odd:P:2].rearrange("p t w -> p (t w)"),
+                        in_=x[b].rearrange("(p two t) h w -> two p (t h w)", two=2, t=PACK)[odd],
+                    )
             else:
                 nc.sync.dma_start(
                     out=raw[b][c][:],
@@ -84,7 +85,8 @@ def tile_simpleconvolution_kernel(tc, x, weight_words, weight_scales, out):
             out_b = out[b].rearrange("(p j) h w -> p j (h w)", j=O_TILES)
             nc.sync.dma_start(out=out_b[:, j_lo:j_hi, :], in_=result[b][:, j_lo:j_hi, :])
 
-        nc.sync.dma_start(out=w_raw[:].bitcast(I32), in_=weight_words[0].bitcast(I32))
+        for odd in range(2):
+            nc.sync.dma_start(out=w_raw[odd:P:2, :].bitcast(I32), in_=weight_words[0].bitcast(I32)[odd:P:2, :])
         load_x(0, 0)
         nc.vector.memset(s_raw[:].bitcast(I32), 0)
         for q in range(4):
@@ -92,7 +94,11 @@ def tile_simpleconvolution_kernel(tc, x, weight_words, weight_scales, out):
                 out=s_raw[32 * q : 32 * q + 4, :].bitcast(I32),
                 in_=weight_scales[0, 4 * q : 4 * q + 4, :].bitcast(I32),
             )
-        load_x(0, 1)
+        for odd in range(2):
+            nc.sync.dma_start(
+                out=raw[0][1][odd:P:2],
+                in_=x[0].rearrange("(p two t) h w -> two p t (h w)", two=2, t=PACK)[odd, :, :, N_TILE:],
+            )
         for b in range(1, B):
             load_x(b, 0)
 

@@ -16,7 +16,7 @@ HALVES = PIX // N_TILE
 O_TILES = COUT // P
 FLOPS = 2 * B * PIX * CIN * COUT
 LOADS = (2, 1, 1, 1)
-STORE_AFTER = ((0, 1, 3), (1, 3), (1, 3), (1, 3))
+STORE_AFTER = ((1, 3), (1, 3), (1, 3), (1, 3))
 
 
 def tile_simpleconvolution_kernel(tc, x, weight_words, weight_scales, out):
@@ -37,10 +37,11 @@ def tile_simpleconvolution_kernel(tc, x, weight_words, weight_scales, out):
         def load_x(b, c):
             width = PIX // LOADS[b]
             if LOADS[b] == 1:
-                for odd in range(2):
+                parts = (1, 1, 4, 4)[b]
+                for part in range(parts):
                     nc.sync.dma_start(
-                        out=raw[b][c][odd:P:2].rearrange("p t w -> p (t w)"),
-                        in_=x[b].rearrange("(p two t) h w -> two p (t h w)", two=2, t=PACK)[odd],
+                        out=raw[b][c][part:P:parts].rearrange("p t w -> p (t w)"),
+                        in_=x[b].rearrange("(p s t) h w -> s p (t h w)", s=parts, t=PACK)[part],
                     )
             else:
                 nc.sync.dma_start(
@@ -85,8 +86,7 @@ def tile_simpleconvolution_kernel(tc, x, weight_words, weight_scales, out):
             out_b = out[b].rearrange("(p j) h w -> p j (h w)", j=O_TILES)
             nc.sync.dma_start(out=out_b[:, j_lo:j_hi, :], in_=result[b][:, j_lo:j_hi, :])
 
-        for odd in range(2):
-            nc.sync.dma_start(out=w_raw[odd:P:2, :].bitcast(I32), in_=weight_words[0].bitcast(I32)[odd:P:2, :])
+        nc.sync.dma_start(out=w_raw[:].bitcast(I32), in_=weight_words[0].bitcast(I32))
         load_x(0, 0)
         nc.vector.memset(s_raw[:].bitcast(I32), 0)
         for q in range(4):
@@ -94,11 +94,7 @@ def tile_simpleconvolution_kernel(tc, x, weight_words, weight_scales, out):
                 out=s_raw[32 * q : 32 * q + 4, :].bitcast(I32),
                 in_=weight_scales[0, 4 * q : 4 * q + 4, :].bitcast(I32),
             )
-        for odd in range(2):
-            nc.sync.dma_start(
-                out=raw[0][1][odd:P:2],
-                in_=x[0].rearrange("(p two t) h w -> two p t (h w)", two=2, t=PACK)[odd, :, :, N_TILE:],
-            )
+        load_x(0, 1)
         for b in range(1, B):
             load_x(b, 0)
 

@@ -16,7 +16,7 @@ HALVES = PIX // N_TILE
 O_TILES = COUT // P
 FLOPS = 2 * B * PIX * CIN * COUT
 LOADS = (2, 1, 1, 1)
-STORE_AFTER = ((1, 3), (1, 3), (1, 3), (1, 3))
+STORE_AFTER = ((1, 3), (1, 3), (1, 3), (3,))
 
 
 def tile_simpleconvolution_kernel(tc, x, weight_words, weight_scales, out):
@@ -102,15 +102,15 @@ def tile_simpleconvolution_kernel(tc, x, weight_words, weight_scales, out):
             out=w_words[:].rearrange("p (j m e) -> p j m e", j=O_TILES, e=2),
             in_=w_raw[:].rearrange("p (m j e) -> p j m e", j=O_TILES, e=2),
         )
-        regroup(nc.scalar.copy, 0, 352, 512)
-        regroup(nc.scalar.copy, 0, 848, 1024)
-        regroup(nc.vector.tensor_copy, 0, 0, 352)
+        regroup(nc.scalar.copy, 0, 368, 512)
+        regroup(nc.scalar.copy, 0, 784, 1024)
+        regroup(nc.vector.tensor_copy, 0, 0, 368)
         nc.vector.tensor_copy(
             out=w_plane[:].rearrange("p (j m) -> p j m", j=O_TILES),
             in_=s_raw[:].rearrange("p (m j) -> p j m", j=O_TILES),
         )
         quantize(0, 0)
-        regroup(nc.vector.tensor_copy, 0, 512, 848)
+        regroup(nc.vector.tensor_copy, 0, 512, 784)
         quantize(0, 1)
 
         for b in range(B):
@@ -122,7 +122,7 @@ def tile_simpleconvolution_kernel(tc, x, weight_words, weight_scales, out):
                     if last:
                         vector_takes = j % 2 == 0
                     else:
-                        vector_takes = b > 0 and pair == 0 and n == 0
+                        vector_takes = b == 1 and pair == 2 and n == 0
                     empty(nc.vector.tensor_copy if vector_takes else nc.scalar.copy, banks[n], b, j, h)
                     if h == 1 and j in STORE_AFTER[b]:
                         store(b, max([0] + [k + 1 for k in STORE_AFTER[b] if k < j]), j + 1)

@@ -26,9 +26,11 @@ def tile_simpleconvolution_kernel(tc, x, weight_words, weight_scales, out):
         w_raw = keep.tile([P, 2 * COUT], U8, name="w_raw", align_bytes=64)
         w_plane = keep.tile([P, COUT], U8, name="w_plane", align_bytes=64)
         w_words = keep.tile([P, 2 * COUT], U8, name="w_words", align_bytes=64)
+        late = keep.tile([P, 2, PACK, PIX], BF16, name="late")
         raw, grouped, codes, plane, result = [], [], [], [], []
         for b in range(B):
-            raw.append([keep.tile([P, PACK, PIX // LOADS[b]], BF16, name="raw%d_%d" % (b, c)) for c in range(LOADS[b])])
+            if b < 2:
+                raw.append([keep.tile([P, PACK, PIX // LOADS[b]], BF16, name="raw%d_%d" % (b, c)) for c in range(LOADS[b])])
             grouped.append(keep.tile([P, PIX, PACK], BF16, name="grouped%d" % b, align_bytes=64))
             codes.append(keep.tile([P, PIX], U32, name="codes%d" % b, align_bytes=64))
             plane.append(keep.tile([P, PIX], U8, name="plane%d" % b, align_bytes=64))
@@ -37,12 +39,10 @@ def tile_simpleconvolution_kernel(tc, x, weight_words, weight_scales, out):
         def load_x(b, c):
             width = PIX // LOADS[b]
             if LOADS[b] == 1:
-                parts = (1, 1, 4, 4)[b]
-                for part in range(parts):
-                    nc.sync.dma_start(
-                        out=raw[b][c][part:P:parts].rearrange("p t w -> p (t w)"),
-                        in_=x[b].rearrange("(p s t) h w -> s p (t h w)", s=parts, t=PACK)[part],
-                    )
+                nc.sync.dma_start(
+                    out=raw[b][c][:].rearrange("p t w -> p (t w)"),
+                    in_=x[b].rearrange("(p t) h w -> p (t h w)", t=PACK),
+                )
             else:
                 nc.sync.dma_start(
                     out=raw[b][c][:],
@@ -52,9 +52,10 @@ def tile_simpleconvolution_kernel(tc, x, weight_words, weight_scales, out):
         def regroup(copy, b, lo, hi):
             width = PIX // LOADS[b]
             c = lo // width
+            source = raw[b][c][:, :, lo - c * width : hi - c * width] if b < 2 else late[:, b - 2, :, lo:hi]
             copy(
                 out=grouped[b][:, lo:hi, :].rearrange("p (c i) t -> p c t i", i=4),
-                in_=raw[b][c][:, :, lo - c * width : hi - c * width].rearrange("p t (c i) -> p c t i", i=4),
+                in_=source.rearrange("p t (c i) -> p c t i", i=4),
             )
 
         def quantize(b, h):
@@ -95,8 +96,11 @@ def tile_simpleconvolution_kernel(tc, x, weight_words, weight_scales, out):
                 in_=weight_scales[0, 4 * q : 4 * q + 4, :].bitcast(I32),
             )
         load_x(0, 1)
-        for b in range(1, B):
-            load_x(b, 0)
+        load_x(1, 0)
+        nc.sync.dma_start(
+            out=late[:].rearrange("p b t w -> p b (t w)"),
+            in_=x[2:4].rearrange("b (p t) h w -> p b (t h w)", t=PACK),
+        )
 
         nc.vector.tensor_copy(
             out=w_words[:].rearrange("p (j m e) -> p j m e", j=O_TILES, e=2),

import concourse.mybir as mybir

BF16 = mybir.dt.bfloat16
F32 = mybir.dt.float32
I32 = mybir.dt.int32
U32 = mybir.dt.uint32
U8 = mybir.dt.uint8
FP8X4 = mybir.dt.float8_e4m3fn_x4
FP4X4 = mybir.dt.float4_e2m1fn_x4

P = 128
PACK = 4
B, CIN, COUT, PIX = 4, 512, 512, 1024
N_TILE = 512
HALVES = PIX // N_TILE
O_TILES = COUT // P
FLOPS = 2 * B * PIX * CIN * COUT
LOADS = (2, 1, 1, 1)
STORE_AFTER = ((1, 3), (1, 3), (1, 3), (3,))


def tile_simpleconvolution_kernel(tc, x, weight_words, weight_scales, out):
    nc = tc.nc
    with tc.tile_pool(name="keep", bufs=1) as keep, tc.psum_pool(name="acc", bufs=8) as acc, tc.manual_schedule():
        s_raw = keep.tile([P, COUT], U8, name="s_raw", align_bytes=64)
        w_raw = keep.tile([P, 2 * COUT], U8, name="w_raw", align_bytes=64)
        w_plane = keep.tile([P, COUT], U8, name="w_plane", align_bytes=64)
        w_words = keep.tile([P, 2 * COUT], U8, name="w_words", align_bytes=64)
        late = keep.tile([P, 2, PACK, PIX], BF16, name="late")
        raw, grouped, codes, plane, result = [], [], [], [], []
        for b in range(B):
            if b < 2:
                raw.append([keep.tile([P, PACK, PIX // LOADS[b]], BF16, name="raw%d_%d" % (b, c)) for c in range(LOADS[b])])
            grouped.append(keep.tile([P, PIX, PACK], BF16, name="grouped%d" % b, align_bytes=64))
            codes.append(keep.tile([P, PIX], U32, name="codes%d" % b, align_bytes=64))
            plane.append(keep.tile([P, PIX], U8, name="plane%d" % b, align_bytes=64))
            result.append(keep.tile([P, O_TILES, PIX], F32, name="result%d" % b))

        def load_x(b, c):
            width = PIX // LOADS[b]
            if LOADS[b] == 1:
                nc.sync.dma_start(
                    out=raw[b][c][:].rearrange("p t w -> p (t w)"),
                    in_=x[b].rearrange("(p t) h w -> p (t h w)", t=PACK),
                )
            else:
                nc.sync.dma_start(
                    out=raw[b][c][:],
                    in_=x[b].rearrange("(p t) h w -> p t (h w)", t=PACK)[:, :, c * width : (c + 1) * width],
                )

        def regroup(copy, b, lo, hi):
            width = PIX // LOADS[b]
            c = lo // width
            source = raw[b][c][:, :, lo - c * width : hi - c * width] if b < 2 else late[:, b - 2, :, lo:hi]
            copy(
                out=grouped[b][:, lo:hi, :].rearrange("p (c i) t -> p c t i", i=4),
                in_=source.rearrange("p t (c i) -> p c t i", i=4),
            )

        def quantize(b, h):
            cols = slice(h * N_TILE, (h + 1) * N_TILE)
            nc.vector.quantize_mx(
                out=codes[b][:, cols].bitcast(FP8X4),
                scales=plane[b][:, cols],
                in_=grouped[b][:, cols, :].rearrange("p w t -> p (w t)"),
            )

        def multiply(b, j, h):
            cols = slice(h * N_TILE, (h + 1) * N_TILE)
            bank = acc.tile([P, N_TILE], F32, name="bank")
            nc.tensor.matmul_mx(
                out=bank[:],
                lhsT=w_words[:, 2 * P * j : 2 * P * (j + 1)].bitcast(FP4X4),
                lhsT_scale=w_plane[:, P * j : P * (j + 1)],
                rhs=codes[b][:, cols].bitcast(FP8X4),
                rhs_scale=plane[b][:, cols],
                start=True,
                stop=True,
            )
            return bank

        def empty(copy, bank, b, j, h):
            copy(out=result[b][:, j, h * N_TILE : (h + 1) * N_TILE], in_=bank[:])

        def store(b, j_lo, j_hi):
            out_b = out[b].rearrange("(p j) h w -> p j (h w)", j=O_TILES)
            nc.sync.dma_start(out=out_b[:, j_lo:j_hi, :], in_=result[b][:, j_lo:j_hi, :])

        nc.sync.dma_start(out=w_raw[:].bitcast(I32), in_=weight_words[0].bitcast(I32))
        load_x(0, 0)
        nc.vector.memset(s_raw[:].bitcast(I32), 0)
        for q in range(4):
            nc.sync.dma_start(
                out=s_raw[32 * q : 32 * q + 4, :].bitcast(I32),
                in_=weight_scales[0, 4 * q : 4 * q + 4, :].bitcast(I32),
            )
        load_x(0, 1)
        load_x(1, 0)
        nc.sync.dma_start(
            out=late[:].rearrange("p b t w -> p b (t w)"),
            in_=x[2:4].rearrange("b (p t) h w -> p b (t h w)", t=PACK),
        )

        nc.vector.tensor_copy(
            out=w_words[:].rearrange("p (j m e) -> p j m e", j=O_TILES, e=2),
            in_=w_raw[:].rearrange("p (m j e) -> p j m e", j=O_TILES, e=2),
        )
        regroup(nc.scalar.copy, 0, 368, 512)
        regroup(nc.scalar.copy, 0, 784, 1024)
        regroup(nc.vector.tensor_copy, 0, 0, 368)
        nc.vector.tensor_copy(
            out=w_plane[:].rearrange("p (j m) -> p j m", j=O_TILES),
            in_=s_raw[:].rearrange("p (m j) -> p j m", j=O_TILES),
        )
        quantize(0, 0)
        regroup(nc.vector.tensor_copy, 0, 512, 784)
        quantize(0, 1)

        for b in range(B):
            last = b == B - 1
            for pair in range(0, O_TILES, 2):
                order = [(pair, 0), (pair + 1, 0), (pair, 1), (pair + 1, 1)]
                banks = [multiply(b, j, h) for j, h in order]
                for n, (j, h) in enumerate(order):
                    if last:
                        vector_takes = j % 2 == 0
                    else:
                        vector_takes = b == 1 and pair == 2 and n == 0
                    empty(nc.vector.tensor_copy if vector_takes else nc.scalar.copy, banks[n], b, j, h)
                    if h == 1 and j in STORE_AFTER[b]:
                        store(b, max([0] + [k + 1 for k in STORE_AFTER[b] if k < j]), j + 1)
                if pair == 0 and not last:
                    regroup(nc.vector.tensor_copy, b + 1, 0, 512)
                    regroup(nc.vector.tensor_copy, b + 1, 512, 1024)
                    quantize(b + 1, 0)
                    quantize(b + 1, 1)
